import numpy as np
import ml_dtypes


def mxq(x, axis, fmt="e4m3"):
    dtype, down = {"e4m3": (ml_dtypes.float8_e4m3fn, 7), "e5m2": (ml_dtypes.float8_e5m2, 14)}[fmt]
    v = np.moveaxis(np.asarray(x, np.float32).astype(ml_dtypes.bfloat16).astype(np.float64), axis, -1)
    blocks = v.reshape(v.shape[:-1] + (-1, 32))
    amax = np.abs(blocks).max(-1, keepdims=True)
    byte = np.maximum(np.where(amax > 0, np.frexp(amax)[1] - 1 + 127, 0) - down, 1)
    scale = np.exp2(byte - 127.0)
    codes = (blocks / scale).astype(np.float32).astype(dtype).astype(np.float64)
    return np.moveaxis((codes * scale).reshape(v.shape), -1, axis)


WIDE = False


def mx_kscale(k):
    if not WIDE:
        return np.ones(k)
    levels = np.array([10, -10, 5, -5, 0])
    a = np.random.permutation(np.resize(levels, k // 512 * 4)).reshape(k // 512, 4)
    idx = np.arange(k)
    return np.exp2(a[idx // 512, idx % 128 // 32])


BF16 = ml_dtypes.bfloat16


def bf(x):
    return np.asarray(x, np.float32).astype(BF16)


def f64(x):
    return np.asarray(x).astype(np.float64)


E2M1 = np.array([0.0, 0.5, 1.0, 1.5, 2.0, 3.0, 4.0, 6.0, -0.0, -0.5, -1.0, -1.5, -2.0, -3.0, -4.0, -6.0])


def pack_weight(w, fmt):
    k, n = w.shape
    w = f64(bf(w)).reshape(k // 32, 32, n)
    amax = np.abs(w).max(1)
    if fmt == "e4m3":
        byte = np.frexp(amax)[1] - 1 + 127 - 7
    else:
        mant, ex = np.frexp(amax / 6.0)
        byte = np.where(mant > 0.5, ex, ex - 1) + 127
    byte = np.clip(np.where(amax > 0, byte, 1), 1, 254)
    scaled = (w * np.exp2(127.0 - byte)[:, None, :]).reshape(k, n).astype(np.float32)
    by_word = np.ascontiguousarray(scaled.reshape(k // 512, 128, 4, n).transpose(0, 1, 3, 2))
    if fmt == "e4m3":
        words = by_word.astype(ml_dtypes.float8_e4m3fn).view(np.uint8)
    else:
        c = by_word.astype(ml_dtypes.float4_e2m1fn).view(np.uint8) & 0xF
        words = c[..., 0::2] | (c[..., 1::2] << 4)
    return np.ascontiguousarray(words), np.ascontiguousarray(byte.astype(np.uint8).reshape(k // 512, 16, n))


def unpack_weight(words, scales, fmt):
    g, p, n, _ = words.shape
    if fmt == "e4m3":
        vals = np.ascontiguousarray(words).view(ml_dtypes.float8_e4m3fn).astype(np.float64)
    else:
        nib = np.empty((g, p, n, 4), np.uint8)
        nib[..., 0::2] = words & 0xF
        nib[..., 1::2] = words >> 4
        vals = E2M1[nib]
    vals = vals * np.repeat(np.exp2(scales.astype(np.float64) - 127.0), 8, axis=1)[..., None]
    return vals.transpose(0, 1, 3, 2).reshape(g * 512, n)


B, N, D = 1, 128, 4096
P0 = 0.2
FMT = "e4m3"


def setup_inputs():
    s = mx_kscale(D)
    g = 0.4 + 1.2 * np.random.random_sample((B, 1, N))
    bound = np.sqrt(6.0 / (D + D))
    embedding = bf(np.random.standard_normal((B, D, N)) * g * np.sqrt(P0) / D ** 0.25 * s[None, :, None])
    heatm = bf(np.random.standard_normal((B, D, N)))
    words, scales = pack_weight(np.random.uniform(-bound, bound, (D, D)) / s[:, None] / s[None, :], FMT)
    return {"embedding": embedding,
            "heatm": heatm,
            "W_b_words": words,
            "W_b_scales": scales}


def reference(embedding, heatm, W_b_words, W_b_scales):
    eq = mxq(f64(embedding), 1, "e4m3")
    t = np.swapaxes(eq, 1, 2) @ unpack_weight(W_b_words, W_b_scales, FMT)
    C = np.tanh(mxq(t, 2, "e4m3") @ eq)
    max_cow = np.max(C, axis=-1, keepdims=True)
    e = np.exp(max_cow - np.max(max_cow, axis=1, keepdims=True))
    return e / np.sum(e, axis=1, keepdims=True)

@@ -1,0 +1,182 @@
+from contextlib import ExitStack
+
+import concourse.mybir as mybir
+from concourse.masks import make_identity
+
+F32 = mybir.dt.float32
+BF16 = mybir.dt.bfloat16
+I32 = mybir.dt.int32
+U32 = mybir.dt.uint32
+U8 = mybir.dt.uint8
+FP8X4 = mybir.dt.float8_e4m3fn_x4
+ACT = mybir.ActivationFunctionType
+ALU = mybir.AluOpType
+AXIS = mybir.AxisListType
+
+P = 128
+PACK = 4
+K_PASS = P * PACK
+D = 4096
+N = 128
+PASSES = D // K_PASS
+BLOCK = 512
+BLOCKS = D // BLOCK
+LATE_PASSES = 2
+EARLY_PASSES = PASSES - LATE_PASSES
+PLANES = 4
+QUADRANT = 32
+COLS_BANKS = 2
+SCORES_BANK = 2
+SPREAD_BANK = 3
+
+FLOPS = 2 * N * D * D + 2 * N * D * N
+BYTES = D * N * 2 + D * D + D * D // 32 + N * 4
+
+
+def tile_parallelcoattention_w_kernel(tc, embedding, heatm, W_b_words, W_b_scales, out):
+    nc = tc.nc
+    with ExitStack() as scope:
+        resident = scope.enter_context(tc.tile_pool(name="resident", bufs=1))
+        stage = scope.enter_context(tc.tile_pool(name="stage", bufs=3))
+        psum = scope.enter_context(tc.psum_pool(name="psum", bufs=1))
+        scope.enter_context(tc.manual_schedule())
+
+        e_raw = resident.tile([P, PASSES, PACK, N], BF16)
+        nc.sync.dma_start(
+            out=e_raw[:], in_=embedding[0].rearrange("(g p j) n -> p g j n", p=P, j=PACK)
+        )
+
+        w_planes = resident.tile([P, PASSES // PLANES, D], U8, align_bytes=64)
+        nc.vector.memset(w_planes[:].bitcast(I32), 0)
+        for group in range(PASSES // PLANES):
+            for quadrant in range(P // QUADRANT):
+                first = QUADRANT * quadrant
+                nc.sync.dma_start(
+                    out=w_planes[first : first + 4 * PLANES, group, :].bitcast(I32),
+                    in_=W_b_scales[
+                        PLANES * group : PLANES * (group + 1), 4 * quadrant : 4 * (quadrant + 1), :
+                    ].bitcast(I32),
+                )
+
+        w_words = {}
+        for g in range(EARLY_PASSES):
+            w_row = resident.tile([P, D], U32, name="w_row%d" % g, align_bytes=64)
+            nc.sync.dma_start(
+                out=w_row[:].bitcast(I32),
+                in_=W_b_words[g].rearrange("p n j -> p (n j)").bitcast(I32),
+            )
+            for c in range(BLOCKS):
+                w_words[(g, c)] = w_row[:, BLOCK * c : BLOCK * (c + 1)]
+        for c in range(BLOCKS):
+            for g in range(EARLY_PASSES, PASSES):
+                w_piece = resident.tile([P, BLOCK], U32, name="w_piece%d_%d" % (g, c), align_bytes=64)
+                nc.sync.dma_start(
+                    out=w_piece[:].bitcast(I32),
+                    in_=W_b_words[g]
+                    .rearrange("p n j -> p (n j)")[:, PACK * BLOCK * c : PACK * BLOCK * (c + 1)]
+                    .bitcast(I32),
+                )
+                w_words[(g, c)] = w_piece[:]
+
+        ident_bf16 = resident.tile([P, P], BF16)
+        make_identity(nc, ident_bf16[:])
+        ident_f32 = resident.tile([P, P], F32)
+        make_identity(nc, ident_f32[:])
+        warm_in = resident.tile([P, 1], F32)
+        nc.vector.memset(warm_in[:], 0.0)
+        warm_out = resident.tile([P, 1], F32)
+        nc.scalar.activation(out=warm_out[:], in_=warm_in[:], func=ACT.Tanh)
+
+        e_grouped = resident.tile([P, PASSES, N, PACK], BF16, align_bytes=64)
+        nc.vector.tensor_copy(out=e_grouped[:], in_=e_raw[:].rearrange("p g j n -> p g n j"))
+        e_codes = resident.tile([P, PASSES, N], U32, align_bytes=64)
+        e_scales = resident.tile([P, PASSES, N], U8, align_bytes=64)
+        nc.vector.quantize_mx(
+            out=e_codes[:].rearrange("p g n -> p (g n)").bitcast(FP8X4),
+            scales=e_scales[:].rearrange("p g n -> p (g n)"),
+            in_=e_grouped[:].rearrange("p g n j -> p (g n j)"),
+        )
+
+        t_banks = [
+            psum.tile([P, BLOCK], F32, name="t_bank%d" % c, tag="bank%d" % c) for c in range(BLOCKS)
+        ]
+
+        def t_pass(g, c):
+            nc.tensor.matmul_mx(
+                out=t_banks[c][:],
+                lhsT=e_codes[:, g, :].bitcast(FP8X4),
+                lhsT_scale=e_scales[:, g, :],
+                rhs=w_words[(g, c)].bitcast(FP8X4),
+                rhs_scale=w_planes[
+                    4 * (g % PLANES) : P, g // PLANES, BLOCK * c : BLOCK * (c + 1)
+                ],
+                start=(g == 0),
+                stop=(g == PASSES - 1),
+            )
+
+        for g in range(EARLY_PASSES):
+            for c in range(BLOCKS):
+                t_pass(g, c)
+
+        t_codes = resident.tile([P, PASSES, N], U32, align_bytes=64)
+        t_scales = resident.tile([P, PASSES, N], U8, align_bytes=64)
+        t_rows = {}
+
+        def finish_block(c):
+            for g in range(EARLY_PASSES, PASSES):
+                t_pass(g, c)
+            rows = stage.tile([P, PACK, P], BF16)
+            nc.scalar.copy(out=rows[:], in_=t_banks[c][:].rearrange("n (p j) -> n j p", j=PACK))
+            t_rows[c] = rows
+
+        def quantise_block(c):
+            cols = psum.tile([P, PACK, N], BF16, tag="bank%d" % (c % COLS_BANKS))
+            for j in range(PACK):
+                nc.tensor.transpose(cols[:, j, :], t_rows[c][:, j, :], ident_bf16[:])
+            grouped = stage.tile([P, N, PACK], BF16, align_bytes=64)
+            nc.vector.tensor_copy(out=grouped[:], in_=cols[:].rearrange("p j n -> p n j"))
+            nc.vector.quantize_mx(
+                out=t_codes[:, c, :].bitcast(FP8X4),
+                scales=t_scales[:, c, :],
+                in_=grouped[:].rearrange("p n j -> p (n j)"),
+            )
+
+        scores = psum.tile([P, N], F32, tag="bank%d" % SCORES_BANK)
+
+        def scores_pass(c):
+            nc.tensor.matmul_mx(
+                out=scores[:],
+                lhsT=t_codes[:, c, :].bitcast(FP8X4),
+                lhsT_scale=t_scales[:, c, :],
+                rhs=e_codes[:, c, :].bitcast(FP8X4),
+                rhs_scale=e_scales[:, c, :],
+                start=(c == 0),
+                stop=(c == BLOCKS - 1),
+            )
+
+        for turn in range(BLOCKS + 2):
+            if turn < BLOCKS:
+                finish_block(turn)
+            if 1 <= turn <= BLOCKS:
+                quantise_block(turn - 1)
+            if turn >= 2:
+                scores_pass(turn - 2)
+
+        row_max = resident.tile([P, 1], F32)
+        nc.vector.reduce_max(out=row_max[:], in_=scores[:], axis=AXIS.X)
+        spread = psum.tile([P, N], F32, tag="bank%d" % SPREAD_BANK)
+        nc.tensor.transpose(spread[:], row_max[:, 0:1].to_broadcast([P, P]), ident_f32[:])
+        c_max = resident.tile([P, N], F32)
+        nc.scalar.activation(out=c_max[:], in_=spread[:], func=ACT.Tanh)
+        neg_top = resident.tile([P, 1], F32)
+        nc.vector.tensor_reduce(out=neg_top[:], in_=c_max[:], axis=AXIS.X, op=ALU.max, negate=True)
+        powers = resident.tile([P, N], F32)
+        total = resident.tile([P, 1], F32)
+        nc.scalar.activation(
+            out=powers[:], in_=c_max[:], func=ACT.Exp, bias=neg_top[:, 0:1], accum_out=total[:]
+        )
+        inverse = resident.tile([P, 1], F32)
+        nc.vector.reciprocal(out=inverse[:], in_=total[:])
+        weights = resident.tile([P, N], F32)
+        nc.vector.tensor_scalar_mul(out=weights[:], in0=powers[:], scalar1=inverse[:, 0:1])
+        nc.sync.dma_start(out=out.rearrange("b n o -> (b o) n"), in_=weights[0:1, :])

@@ -21,13 +21,15 @@ N = 128
 PASSES = D // K_PASS
 BLOCK = 512
 BLOCKS = D // BLOCK
-LATE_PASSES = 2
+GROUP_BLOCKS = 2
+GROUPS = BLOCKS // GROUP_BLOCKS
+GROUP = GROUP_BLOCKS * BLOCK
+LATE_PASSES = 4
 EARLY_PASSES = PASSES - LATE_PASSES
+TRANSPOSES_AFTER = 0
+SCORES_AFTER = 2
 PLANES = 4
 QUADRANT = 32
-COLS_BANKS = 2
-SCORES_BANK = 2
-SPREAD_BANK = 3
 
 FLOPS = 2 * N * D * D + 2 * N * D * N
 BYTES = D * N * 2 + D * D + D * D // 32 + N * 4
@@ -37,7 +39,7 @@ def tile_parallelcoattention_w_kernel(tc, embedding, heatm, W_b_words, W_b_scale
     nc = tc.nc
     with ExitStack() as scope:
         resident = scope.enter_context(tc.tile_pool(name="resident", bufs=1))
-        stage = scope.enter_context(tc.tile_pool(name="stage", bufs=3))
+        stage = scope.enter_context(tc.tile_pool(name="stage", bufs=2))
         psum = scope.enter_context(tc.psum_pool(name="psum", bufs=1))
         scope.enter_context(tc.manual_schedule())
 
@@ -48,13 +50,13 @@ def tile_parallelcoattention_w_kernel(tc, embedding, heatm, W_b_words, W_b_scale
 
         w_planes = resident.tile([P, PASSES // PLANES, D], U8, align_bytes=64)
         nc.vector.memset(w_planes[:].bitcast(I32), 0)
-        for group in range(PASSES // PLANES):
+        for four in range(PASSES // PLANES):
             for quadrant in range(P // QUADRANT):
                 first = QUADRANT * quadrant
                 nc.sync.dma_start(
-                    out=w_planes[first : first + 4 * PLANES, group, :].bitcast(I32),
+                    out=w_planes[first : first + 4 * PLANES, four, :].bitcast(I32),
                     in_=W_b_scales[
-                        PLANES * group : PLANES * (group + 1), 4 * quadrant : 4 * (quadrant + 1), :
+                        PLANES * four : PLANES * (four + 1), 4 * quadrant : 4 * (quadrant + 1), :
                     ].bitcast(I32),
                 )
 
@@ -67,16 +69,17 @@ def tile_parallelcoattention_w_kernel(tc, embedding, heatm, W_b_words, W_b_scale
             )
             for c in range(BLOCKS):
                 w_words[(g, c)] = w_row[:, BLOCK * c : BLOCK * (c + 1)]
-        for c in range(BLOCKS):
+        for q in range(GROUPS):
             for g in range(EARLY_PASSES, PASSES):
-                w_piece = resident.tile([P, BLOCK], U32, name="w_piece%d_%d" % (g, c), align_bytes=64)
+                w_piece = resident.tile([P, GROUP], U32, name="w_piece%d_%d" % (g, q), align_bytes=64)
                 nc.sync.dma_start(
                     out=w_piece[:].bitcast(I32),
                     in_=W_b_words[g]
-                    .rearrange("p n j -> p (n j)")[:, PACK * BLOCK * c : PACK * BLOCK * (c + 1)]
+                    .rearrange("p n j -> p (n j)")[:, PACK * GROUP * q : PACK * GROUP * (q + 1)]
                     .bitcast(I32),
                 )
-                w_words[(g, c)] = w_piece[:]
+                for b in range(GROUP_BLOCKS):
+                    w_words[(g, GROUP_BLOCKS * q + b)] = w_piece[:, BLOCK * b : BLOCK * (b + 1)]
 
         ident_bf16 = resident.tile([P, P], BF16)
         make_identity(nc, ident_bf16[:])
@@ -100,6 +103,9 @@ def tile_parallelcoattention_w_kernel(tc, embedding, heatm, W_b_words, W_b_scale
         t_banks = [
             psum.tile([P, BLOCK], F32, name="t_bank%d" % c, tag="bank%d" % c) for c in range(BLOCKS)
         ]
+        t_codes = resident.tile([P, PASSES, N], U32, align_bytes=64)
+        t_scales = resident.tile([P, PASSES, N], U8, align_bytes=64)
+        t_rows = {}
 
         def t_pass(g, c):
             nc.tensor.matmul_mx(
@@ -114,36 +120,37 @@ def tile_parallelcoattention_w_kernel(tc, embedding, heatm, W_b_words, W_b_scale
                 stop=(g == PASSES - 1),
             )
 
-        for g in range(EARLY_PASSES):
-            for c in range(BLOCKS):
-                t_pass(g, c)
+        def leave_psum(c, out_tile, in_bank):
+            if c % 2 == 0:
+                nc.scalar.copy(out=out_tile, in_=in_bank)
+            else:
+                nc.vector.tensor_copy(out=out_tile, in_=in_bank)
 
-        t_codes = resident.tile([P, PASSES, N], U32, align_bytes=64)
-        t_scales = resident.tile([P, PASSES, N], U8, align_bytes=64)
-        t_rows = {}
+        def round_group(q):
+            for c in range(GROUP_BLOCKS * q, GROUP_BLOCKS * (q + 1)):
+                rows = stage.tile([P, PACK, P], BF16, name="rows%d" % (c % GROUP_BLOCKS))
+                leave_psum(c, rows[:], t_banks[c][:].rearrange("n (p j) -> n j p", j=PACK))
+                t_rows[c] = rows
 
-        def finish_block(c):
-            for g in range(EARLY_PASSES, PASSES):
-                t_pass(g, c)
-            rows = stage.tile([P, PACK, P], BF16)
-            nc.scalar.copy(out=rows[:], in_=t_banks[c][:].rearrange("n (p j) -> n j p", j=PACK))
-            t_rows[c] = rows
-
-        def quantise_block(c):
-            cols = psum.tile([P, PACK, N], BF16, tag="bank%d" % (c % COLS_BANKS))
-            for j in range(PACK):
-                nc.tensor.transpose(cols[:, j, :], t_rows[c][:, j, :], ident_bf16[:])
-            grouped = stage.tile([P, N, PACK], BF16, align_bytes=64)
-            nc.vector.tensor_copy(out=grouped[:], in_=cols[:].rearrange("p j n -> p n j"))
+        def quantise_group(q):
+            grouped = stage.tile([P, GROUP_BLOCKS, N, PACK], BF16, align_bytes=64)
+            first = GROUP_BLOCKS * q
+            cols = {}
+            for c in range(first, first + GROUP_BLOCKS):
+                cols[c] = psum.tile([P, PACK, N], BF16, name="cols%d" % c, tag="bank%d" % c)
+                for j in range(PACK):
+                    nc.tensor.transpose(cols[c][:, j, :], t_rows[c][:, j, :], ident_bf16[:])
+            for c in range(first, first + GROUP_BLOCKS):
+                leave_psum(c, grouped[:, c - first], cols[c][:].rearrange("p j n -> p n j"))
             nc.vector.quantize_mx(
-                out=t_codes[:, c, :].bitcast(FP8X4),
-                scales=t_scales[:, c, :],
-                in_=grouped[:].rearrange("p n j -> p (n j)"),
+                out=t_codes[:, first : first + GROUP_BLOCKS, :]
+                .rearrange("p c n -> p (c n)")
+                .bitcast(FP8X4),
+                scales=t_scales[:, first : first + GROUP_BLOCKS, :].rearrange("p c n -> p (c n)"),
+                in_=grouped[:].rearrange("p c n j -> p (c n j)"),
             )
 
-        scores = psum.tile([P, N], F32, tag="bank%d" % SCORES_BANK)
-
-        def scores_pass(c):
+        def scores_pass(scores, c):
             nc.tensor.matmul_mx(
                 out=scores[:],
                 lhsT=t_codes[:, c, :].bitcast(FP8X4),
@@ -154,17 +161,29 @@ def tile_parallelcoattention_w_kernel(tc, embedding, heatm, W_b_words, W_b_scale
                 stop=(c == BLOCKS - 1),
             )
 
-        for turn in range(BLOCKS + 2):
-            if turn < BLOCKS:
-                finish_block(turn)
-            if 1 <= turn <= BLOCKS:
-                quantise_block(turn - 1)
-            if turn >= 2:
-                scores_pass(turn - 2)
+        for g in range(EARLY_PASSES):
+            for c in range(BLOCKS):
+                t_pass(g, c)
+
+        scores = None
+        for q in range(GROUPS + 1):
+            for late in range(LATE_PASSES):
+                if q < GROUPS:
+                    for c in range(GROUP_BLOCKS * q, GROUP_BLOCKS * (q + 1)):
+                        t_pass(EARLY_PASSES + late, c)
+                if q > 0 and late == TRANSPOSES_AFTER:
+                    quantise_group(q - 1)
+                if q > 0 and late == SCORES_AFTER:
+                    if scores is None:
+                        scores = psum.tile([P, N], F32, tag="bank0")
+                    for c in range(GROUP_BLOCKS * (q - 1), GROUP_BLOCKS * q):
+                        scores_pass(scores, c)
+            if q < GROUPS:
+                round_group(q)
 
         row_max = resident.tile([P, 1], F32)
         nc.vector.reduce_max(out=row_max[:], in_=scores[:], axis=AXIS.X)
-        spread = psum.tile([P, N], F32, tag="bank%d" % SPREAD_BANK)
+        spread = psum.tile([P, N], F32, tag="bank1")
         nc.tensor.transpose(spread[:], row_max[:, 0:1].to_broadcast([P, P]), ident_f32[:])
         c_max = resident.tile([P, N], F32)
         nc.scalar.activation(out=c_max[:], in_=spread[:], func=ACT.Tanh)

@@ -71,15 +71,22 @@ def tile_parallelcoattention_w_kernel(tc, embedding, heatm, W_b_words, W_b_scale
                 w_words[(g, c)] = w_row[:, BLOCK * c : BLOCK * (c + 1)]
         for q in range(GROUPS):
             for g in range(EARLY_PASSES, PASSES):
-                w_piece = resident.tile([P, GROUP], U32, name="w_piece%d_%d" % (g, q), align_bytes=64)
-                nc.sync.dma_start(
-                    out=w_piece[:].bitcast(I32),
-                    in_=W_b_words[g]
-                    .rearrange("p n j -> p (n j)")[:, PACK * GROUP * q : PACK * GROUP * (q + 1)]
-                    .bitcast(I32),
-                )
-                for b in range(GROUP_BLOCKS):
-                    w_words[(g, GROUP_BLOCKS * q + b)] = w_piece[:, BLOCK * b : BLOCK * (b + 1)]
+                very_last = q == GROUPS - 1 and g == PASSES - 1
+                piece_blocks = 1 if very_last else GROUP_BLOCKS
+                for first in range(GROUP_BLOCKS * q, GROUP_BLOCKS * (q + 1), piece_blocks):
+                    w_piece = resident.tile(
+                        [P, BLOCK * piece_blocks], U32, name="w_piece%d_%d" % (g, first), align_bytes=64
+                    )
+                    nc.sync.dma_start(
+                        out=w_piece[:].bitcast(I32),
+                        in_=W_b_words[g]
+                        .rearrange("p n j -> p (n j)")[
+                            :, PACK * BLOCK * first : PACK * BLOCK * (first + piece_blocks)
+                        ]
+                        .bitcast(I32),
+                    )
+                    for b in range(piece_blocks):
+                        w_words[(g, first + b)] = w_piece[:, BLOCK * b : BLOCK * (b + 1)]
 
         ident_bf16 = resident.tile([P, P], BF16)
         make_identity(nc, ident_bf16[:])
@@ -166,11 +173,10 @@ def tile_parallelcoattention_w_kernel(tc, embedding, heatm, W_b_words, W_b_scale
                 t_pass(g, c)
 
         scores = None
-        for q in range(GROUPS + 1):
+        for q in range(GROUPS):
             for late in range(LATE_PASSES):
-                if q < GROUPS:
-                    for c in range(GROUP_BLOCKS * q, GROUP_BLOCKS * (q + 1)):
-                        t_pass(EARLY_PASSES + late, c)
+                for c in range(GROUP_BLOCKS * q, GROUP_BLOCKS * (q + 1)):
+                    t_pass(EARLY_PASSES + late, c)
                 if q > 0 and late == TRANSPOSES_AFTER:
                     quantise_group(q - 1)
                 if q > 0 and late == SCORES_AFTER:
@@ -178,8 +184,35 @@ def tile_parallelcoattention_w_kernel(tc, embedding, heatm, W_b_words, W_b_scale
                         scores = psum.tile([P, N], F32, tag="bank0")
                     for c in range(GROUP_BLOCKS * (q - 1), GROUP_BLOCKS * q):
                         scores_pass(scores, c)
-            if q < GROUPS:
+            if q < GROUPS - 1:
                 round_group(q)
+
+        c_a, c_b = BLOCKS - 2, BLOCKS - 1
+        rows_a = stage.tile([P, PACK, P], BF16, name="rows0")
+        rows_b = stage.tile([P, PACK, P], BF16, name="rows1")
+        sums_a = t_banks[c_a][:].rearrange("n (p j) -> n j p", j=PACK)
+        sums_b = t_banks[c_b][:].rearrange("n (p j) -> n j p", j=PACK)
+        nc.scalar.copy(out=rows_a[:], in_=sums_a)
+        nc.vector.tensor_copy(out=rows_b[:, 0:2, :], in_=sums_b[:, 0:2, :])
+        nc.vector.tensor_copy(out=rows_b[:, 2:4, :], in_=sums_b[:, 2:4, :])
+        cols_a = psum.tile([P, PACK, N], BF16, name="cols_a", tag="bank%d" % c_a)
+        cols_b = psum.tile([P, PACK, N], BF16, name="cols_b", tag="bank%d" % (c_b - 3))
+        for j in range(PACK):
+            nc.tensor.transpose(cols_a[:, j, :], rows_a[:, j, :], ident_bf16[:])
+        for j in range(PACK):
+            nc.tensor.transpose(cols_b[:, j, :], rows_b[:, j, :], ident_bf16[:])
+        grouped_a = resident.tile([P, N, PACK], BF16, align_bytes=64)
+        grouped_b = resident.tile([P, N, PACK], BF16, align_bytes=64)
+        nc.scalar.copy(out=grouped_a[:], in_=cols_a[:].rearrange("p j n -> p n j"))
+        nc.vector.tensor_copy(out=grouped_b[:], in_=cols_b[:].rearrange("p j n -> p n j"))
+        for c, grouped in ((c_a, grouped_a), (c_b, grouped_b)):
+            nc.vector.quantize_mx(
+                out=t_codes[:, c, :].bitcast(FP8X4),
+                scales=t_scales[:, c, :],
+                in_=grouped[:].rearrange("p n j -> p (n j)"),
+            )
+        scores_pass(scores, c_a)
+        scores_pass(scores, c_b)
 
         row_max = resident.tile([P, 1], F32)
         nc.vector.reduce_max(out=row_max[:], in_=scores[:], axis=AXIS.X)

@@ -15,19 +15,17 @@ AXIS = mybir.AxisListType
 
 P = 128
 PACK = 4
+HALVES = 2
 K_PASS = P * PACK
 D = 4096
 N = 128
 PASSES = D // K_PASS
 BLOCK = 512
 BLOCKS = D // BLOCK
-GROUP_BLOCKS = 2
-GROUPS = BLOCKS // GROUP_BLOCKS
-GROUP = GROUP_BLOCKS * BLOCK
-LATE_PASSES = 4
+PAIR = 2
+LATE_PASSES = 3
 EARLY_PASSES = PASSES - LATE_PASSES
-TRANSPOSES_AFTER = 0
-SCORES_AFTER = 2
+LATE_GROUPS = ((0, 1, 2, 3), (4, 5), (6, 7))
 PLANES = 4
 QUADRANT = 32
 
@@ -69,11 +67,11 @@ def tile_parallelcoattention_w_kernel(tc, embedding, heatm, W_b_words, W_b_scale
             )
             for c in range(BLOCKS):
                 w_words[(g, c)] = w_row[:, BLOCK * c : BLOCK * (c + 1)]
-        for q in range(GROUPS):
+        for group in LATE_GROUPS:
             for g in range(EARLY_PASSES, PASSES):
-                very_last = q == GROUPS - 1 and g == PASSES - 1
-                piece_blocks = 1 if very_last else GROUP_BLOCKS
-                for first in range(GROUP_BLOCKS * q, GROUP_BLOCKS * (q + 1), piece_blocks):
+                very_last = group == LATE_GROUPS[-1] and g == PASSES - 1
+                piece_blocks = 1 if very_last else len(group)
+                for first in range(group[0], group[-1] + 1, piece_blocks):
                     w_piece = resident.tile(
                         [P, BLOCK * piece_blocks], U32, name="w_piece%d_%d" % (g, first), align_bytes=64
                     )
@@ -88,8 +86,6 @@ def tile_parallelcoattention_w_kernel(tc, embedding, heatm, W_b_words, W_b_scale
                     for b in range(piece_blocks):
                         w_words[(g, first + b)] = w_piece[:, BLOCK * b : BLOCK * (b + 1)]
 
-        ident_bf16 = resident.tile([P, P], BF16)
-        make_identity(nc, ident_bf16[:])
         ident_f32 = resident.tile([P, P], F32)
         make_identity(nc, ident_f32[:])
         warm_in = resident.tile([P, 1], F32)
@@ -127,33 +123,39 @@ def tile_parallelcoattention_w_kernel(tc, embedding, heatm, W_b_words, W_b_scale
                 stop=(g == PASSES - 1),
             )
 
+        def words_of(pairs):
+            return pairs.rearrange("p x i -> p (x i)").bitcast(F32)
+
         def leave_psum(c, out_tile, in_bank):
             if c % 2 == 0:
                 nc.scalar.copy(out=out_tile, in_=in_bank)
             else:
                 nc.vector.tensor_copy(out=out_tile, in_=in_bank)
 
-        def round_group(q):
-            for c in range(GROUP_BLOCKS * q, GROUP_BLOCKS * (q + 1)):
-                rows = stage.tile([P, PACK, P], BF16, name="rows%d" % (c % GROUP_BLOCKS))
-                leave_psum(c, rows[:], t_banks[c][:].rearrange("n (p j) -> n j p", j=PACK))
+        def round_pair(first):
+            for c in range(first, first + PAIR):
+                rows = stage.tile([P, HALVES, P, 2], BF16, name="rows%d" % (c % PAIR))
+                leave_psum(c, rows[:], t_banks[c][:].rearrange("n (p u i) -> n u p i", u=HALVES, i=2))
                 t_rows[c] = rows
 
-        def quantise_group(q):
-            grouped = stage.tile([P, GROUP_BLOCKS, N, PACK], BF16, align_bytes=64)
-            first = GROUP_BLOCKS * q
+        def quantise_pair(first):
+            grouped = stage.tile([P, PAIR, N, PACK], BF16, align_bytes=64)
             cols = {}
-            for c in range(first, first + GROUP_BLOCKS):
-                cols[c] = psum.tile([P, PACK, N], BF16, name="cols%d" % c, tag="bank%d" % c)
-                for j in range(PACK):
-                    nc.tensor.transpose(cols[c][:, j, :], t_rows[c][:, j, :], ident_bf16[:])
-            for c in range(first, first + GROUP_BLOCKS):
-                leave_psum(c, grouped[:, c - first], cols[c][:].rearrange("p j n -> p n j"))
+            for c in range(first, first + PAIR):
+                cols[c] = psum.tile([P, HALVES, N], F32, name="cols%d" % c, tag="bank%d" % c)
+                for u in range(HALVES):
+                    nc.tensor.transpose(cols[c][:, u, :], words_of(t_rows[c][:, u]), ident_f32[:])
+            for c in range(first, first + PAIR):
+                leave_psum(
+                    c,
+                    words_of(grouped[:, c - first]).rearrange("p (n u) -> p n u", u=HALVES),
+                    cols[c][:].rearrange("p u n -> p n u"),
+                )
             nc.vector.quantize_mx(
-                out=t_codes[:, first : first + GROUP_BLOCKS, :]
+                out=t_codes[:, first : first + PAIR, :]
                 .rearrange("p c n -> p (c n)")
                 .bitcast(FP8X4),
-                scales=t_scales[:, first : first + GROUP_BLOCKS, :].rearrange("p c n -> p (c n)"),
+                scales=t_scales[:, first : first + PAIR, :].rearrange("p c n -> p (c n)"),
                 in_=grouped[:].rearrange("p c n j -> p (c n j)"),
             )
 
@@ -172,39 +174,58 @@ def tile_parallelcoattention_w_kernel(tc, embedding, heatm, W_b_words, W_b_scale
             for c in range(BLOCKS):
                 t_pass(g, c)
 
-        scores = None
-        for q in range(GROUPS):
+        score_tiles = []
+
+        def scores_pair(first):
+            if not score_tiles:
+                score_tiles.append(psum.tile([P, N], F32, name="scores", tag="bank0"))
+            for c in range(first, first + PAIR):
+                scores_pass(score_tiles[0], c)
+
+        owed = []
+        for group in LATE_GROUPS:
             for late in range(LATE_PASSES):
-                for c in range(GROUP_BLOCKS * q, GROUP_BLOCKS * (q + 1)):
+                for c in group:
                     t_pass(EARLY_PASSES + late, c)
-                if q > 0 and late == TRANSPOSES_AFTER:
-                    quantise_group(q - 1)
-                if q > 0 and late == SCORES_AFTER:
-                    if scores is None:
-                        scores = psum.tile([P, N], F32, tag="bank0")
-                    for c in range(GROUP_BLOCKS * (q - 1), GROUP_BLOCKS * q):
-                        scores_pass(scores, c)
-            if q < GROUPS - 1:
-                round_group(q)
+                very_last = group == LATE_GROUPS[-1] and late == LATE_PASSES - 1
+                for step, first in owed[: len(owed) if very_last else 1]:
+                    step(first)
+                owed = [] if very_last else owed[1:]
+            if group != LATE_GROUPS[-1]:
+                for first in group[::PAIR]:
+                    round_pair(first)
+                owed = (
+                    [item for item in owed if item[0] == quantise_pair]
+                    + [(quantise_pair, first) for first in group[::PAIR]]
+                    + [item for item in owed if item[0] == scores_pair]
+                    + [(scores_pair, first) for first in group[::PAIR]]
+                )
+        scores = score_tiles[0]
 
         c_a, c_b = BLOCKS - 2, BLOCKS - 1
-        rows_a = stage.tile([P, PACK, P], BF16, name="rows0")
-        rows_b = stage.tile([P, PACK, P], BF16, name="rows1")
-        sums_a = t_banks[c_a][:].rearrange("n (p j) -> n j p", j=PACK)
-        sums_b = t_banks[c_b][:].rearrange("n (p j) -> n j p", j=PACK)
+        rows_a = stage.tile([P, HALVES, P, 2], BF16, name="rows0")
+        rows_b = stage.tile([P, HALVES, P, 2], BF16, name="rows1")
+        sums_a = t_banks[c_a][:].rearrange("n (p u i) -> n u p i", u=HALVES, i=2)
+        sums_b = t_banks[c_b][:].rearrange("n (p u i) -> n u p i", u=HALVES, i=2)
         nc.scalar.copy(out=rows_a[:], in_=sums_a)
-        nc.vector.tensor_copy(out=rows_b[:, 0:2, :], in_=sums_b[:, 0:2, :])
-        nc.vector.tensor_copy(out=rows_b[:, 2:4, :], in_=sums_b[:, 2:4, :])
-        cols_a = psum.tile([P, PACK, N], BF16, name="cols_a", tag="bank%d" % c_a)
-        cols_b = psum.tile([P, PACK, N], BF16, name="cols_b", tag="bank%d" % (c_b - 3))
-        for j in range(PACK):
-            nc.tensor.transpose(cols_a[:, j, :], rows_a[:, j, :], ident_bf16[:])
-        for j in range(PACK):
-            nc.tensor.transpose(cols_b[:, j, :], rows_b[:, j, :], ident_bf16[:])
+        for u in range(HALVES):
+            nc.vector.tensor_copy(out=rows_b[:, u], in_=sums_b[:, u])
+        cols_a = psum.tile([P, HALVES, N], F32, name="cols_a", tag="bank%d" % c_a)
+        cols_b = psum.tile([P, HALVES, N], F32, name="cols_b", tag="bank%d" % (c_b - 3))
+        for u in range(HALVES):
+            nc.tensor.transpose(cols_a[:, u, :], words_of(rows_a[:, u]), ident_f32[:])
+        for u in range(HALVES):
+            nc.tensor.transpose(cols_b[:, u, :], words_of(rows_b[:, u]), ident_f32[:])
         grouped_a = resident.tile([P, N, PACK], BF16, align_bytes=64)
         grouped_b = resident.tile([P, N, PACK], BF16, align_bytes=64)
-        nc.scalar.copy(out=grouped_a[:], in_=cols_a[:].rearrange("p j n -> p n j"))
-        nc.vector.tensor_copy(out=grouped_b[:], in_=cols_b[:].rearrange("p j n -> p n j"))
+        nc.scalar.copy(
+            out=words_of(grouped_a[:]).rearrange("p (n u) -> p n u", u=HALVES),
+            in_=cols_a[:].rearrange("p u n -> p n u"),
+        )
+        nc.vector.tensor_copy(
+            out=words_of(grouped_b[:]).rearrange("p (n u) -> p n u", u=HALVES),
+            in_=cols_b[:].rearrange("p u n -> p n u"),
+        )
         for c, grouped in ((c_a, grouped_a), (c_b, grouped_b)):
             nc.vector.quantize_mx(
                 out=t_codes[:, c, :].bitcast(FP8X4),
@@ -216,12 +237,18 @@ def tile_parallelcoattention_w_kernel(tc, embedding, heatm, W_b_words, W_b_scale
 
         row_max = resident.tile([P, 1], F32)
         nc.vector.reduce_max(out=row_max[:], in_=scores[:], axis=AXIS.X)
-        spread = psum.tile([P, N], F32, tag="bank1")
-        nc.tensor.transpose(spread[:], row_max[:, 0:1].to_broadcast([P, P]), ident_f32[:])
+        spread_v = psum.tile([P, N], F32, tag="bank1")
+        spread_s = psum.tile([P, N], F32, tag="bank2")
+        nc.tensor.transpose(spread_v[:], row_max[:, 0:1].to_broadcast([P, P]), ident_f32[:])
+        nc.tensor.transpose(spread_s[:], row_max[:, 0:1].to_broadcast([P, P]), ident_f32[:])
+        neg_raw_top = resident.tile([P, 1], F32)
+        nc.vector.tensor_reduce(
+            out=neg_raw_top[:], in_=spread_v[:], axis=AXIS.X, op=ALU.max, negate=True
+        )
         c_max = resident.tile([P, N], F32)
-        nc.scalar.activation(out=c_max[:], in_=spread[:], func=ACT.Tanh)
+        nc.scalar.activation(out=c_max[:], in_=spread_s[:], func=ACT.Tanh)
         neg_top = resident.tile([P, 1], F32)
-        nc.vector.tensor_reduce(out=neg_top[:], in_=c_max[:], axis=AXIS.X, op=ALU.max, negate=True)
+        nc.scalar.activation(out=neg_top[:], in_=neg_raw_top[:], func=ACT.Tanh)
         powers = resident.tile([P, N], F32)
         total = resident.tile([P, 1], F32)
         nc.scalar.activation(

@@ -26,6 +26,8 @@ PAIR = 2
 LATE_PASSES = 3
 EARLY_PASSES = PASSES - LATE_PASSES
 LATE_GROUPS = ((0, 1, 2, 3), (4, 5), (6, 7))
+ROWS_LONG = D // P
+PAIRS_LONG = ROWS_LONG // 2
 PLANES = 4
 QUADRANT = 32
 
@@ -41,10 +43,8 @@ def tile_parallelcoattention_w_kernel(tc, embedding, heatm, W_b_words, W_b_scale
         psum = scope.enter_context(tc.psum_pool(name="psum", bufs=1))
         scope.enter_context(tc.manual_schedule())
 
-        e_raw = resident.tile([P, PASSES, PACK, N], BF16)
-        nc.sync.dma_start(
-            out=e_raw[:], in_=embedding[0].rearrange("(g p j) n -> p g j n", p=P, j=PACK)
-        )
+        e_long = resident.tile([P, ROWS_LONG, N], BF16)
+        nc.sync.dma_start(out=e_long[:], in_=embedding[0].rearrange("(q r) n -> q r n", q=P))
 
         w_planes = resident.tile([P, PASSES // PLANES, D], U8, align_bytes=64)
         nc.vector.memset(w_planes[:].bitcast(I32), 0)
@@ -93,8 +93,36 @@ def tile_parallelcoattention_w_kernel(tc, embedding, heatm, W_b_words, W_b_scale
         warm_out = resident.tile([P, 1], F32)
         nc.scalar.activation(out=warm_out[:], in_=warm_in[:], func=ACT.Tanh)
 
+        e_words = e_long[:].rearrange("q r n -> q (r n)").bitcast(F32)
+        e_turned = resident.tile([P, P, PAIRS_LONG], F32)
+        for b in range(PAIRS_LONG // PACK):
+            turned = psum.tile([P, PACK, P], F32, name="turned%d" % b, tag="bank%d" % b)
+            for k in range(PACK):
+                first_word = P * (PACK * b + k)
+                nc.tensor.transpose(turned[:, k, :], e_words[:, first_word : first_word + P], ident_f32[:])
+            copy_out = nc.scalar.copy if b % 2 == 0 else nc.vector.tensor_copy
+            copy_out(
+                out=e_turned[:, :, PACK * b : PACK * (b + 1)], in_=turned[:].rearrange("x k q -> x q k")
+            )
+        e_flat = e_turned[:].rearrange("x q k -> x (q k)")
         e_grouped = resident.tile([P, PASSES, N, PACK], BF16, align_bytes=64)
-        nc.vector.tensor_copy(out=e_grouped[:], in_=e_raw[:].rearrange("p g j n -> p g n j"))
+        for b in range(PASSES // 2):
+            placed = psum.tile([P, 2, HALVES, P], F32, name="placed%d" % b, tag="bank%d" % (4 + b))
+            for g in range(2):
+                for u in range(HALVES):
+                    first_word = 2 * P * (2 * b + g) + u
+                    nc.tensor.transpose(
+                        placed[:, g, u, :], e_flat[:, first_word : first_word + 2 * P - 1 : 2], ident_f32[:]
+                    )
+            copy_out = nc.scalar.copy if b % 2 == 0 else nc.vector.tensor_copy
+            copy_out(
+                out=e_grouped[:, 2 * b : 2 * b + 2],
+                in_=placed[:]
+                .rearrange("p g u x -> p (g u x)")
+                .bitcast(BF16)
+                .rearrange("p (g j n) -> p g n j", g=2, j=PACK),
+            )
+
         e_codes = resident.tile([P, PASSES, N], U32, align_bytes=64)
         e_scales = resident.tile([P, PASSES, N], U8, align_bytes=64)
         nc.vector.quantize_mx(

@@ -51,12 +51,14 @@ def tile_parallelcoattention_w_kernel(tc, embedding, heatm, W_b_words, W_b_scale
         for four in range(PASSES // PLANES):
             for quadrant in range(P // QUADRANT):
                 first = QUADRANT * quadrant
-                nc.sync.dma_start(
-                    out=w_planes[first : first + 4 * PLANES, four, :].bitcast(I32),
-                    in_=W_b_scales[
-                        PLANES * four : PLANES * (four + 1), 4 * quadrant : 4 * (quadrant + 1), :
-                    ].bitcast(I32),
-                )
+                for half in range(2):
+                    cols = slice(half * D // 2, (half + 1) * D // 2)
+                    nc.sync.dma_start(
+                        out=w_planes[first : first + 4 * PLANES, four, cols].bitcast(I32),
+                        in_=W_b_scales[
+                            PLANES * four : PLANES * (four + 1), 4 * quadrant : 4 * (quadrant + 1), cols
+                        ].bitcast(I32),
+                    )
 
         w_words = {}
         for g in range(EARLY_PASSES):

@@ -43,13 +43,16 @@ def tile_parallelcoattention_w_kernel(tc, embedding, heatm, W_b_words, W_b_scale
         psum = scope.enter_context(tc.psum_pool(name="psum", bufs=1))
         scope.enter_context(tc.manual_schedule())
 
+        ident_f32 = resident.tile([P, P], F32)
+        make_identity(nc, ident_f32[:])
+
         e_long = resident.tile([P, ROWS_LONG, N], BF16)
         nc.sync.dma_start(out=e_long[:], in_=embedding[0].rearrange("(q r) n -> q r n", q=P))
 
         w_planes = resident.tile([P, PASSES // PLANES, D], U8, align_bytes=64)
         nc.vector.memset(w_planes[:].bitcast(I32), 0)
         for four in range(PASSES // PLANES):
-            for quadrant in range(P // QUADRANT):
+            for quadrant in (0, 1):
                 first = QUADRANT * quadrant
                 for half in range(2):
                     cols = slice(half * D // 2, (half + 1) * D // 2)
@@ -59,6 +62,15 @@ def tile_parallelcoattention_w_kernel(tc, embedding, heatm, W_b_words, W_b_scale
                             PLANES * four : PLANES * (four + 1), 4 * quadrant : 4 * (quadrant + 1), cols
                         ].bitcast(I32),
                     )
+        for four in range(PASSES // PLANES):
+            for quadrant in (2, 3):
+                first = QUADRANT * quadrant
+                nc.gpsimd.dma_start(
+                    out=w_planes[first : first + 4 * PLANES, four, :].bitcast(F32),
+                    in_=W_b_scales[
+                        PLANES * four : PLANES * (four + 1), 4 * quadrant : 4 * (quadrant + 1), :
+                    ].bitcast(F32),
+                )
 
         w_words = {}
         for g in range(EARLY_PASSES):
@@ -88,8 +100,6 @@ def tile_parallelcoattention_w_kernel(tc, embedding, heatm, W_b_words, W_b_scale
                     for b in range(piece_blocks):
                         w_words[(g, first + b)] = w_piece[:, BLOCK * b : BLOCK * (b + 1)]
 
-        ident_f32 = resident.tile([P, P], F32)
-        make_identity(nc, ident_f32[:])
         warm_in = resident.tile([P, 1], F32)
         nc.vector.memset(warm_in[:], 0.0)
         warm_out = resident.tile([P, 1], F32)

@@ -43,14 +43,26 @@ def tile_parallelcoattention_w_kernel(tc, embedding, heatm, W_b_words, W_b_scale
         psum = scope.enter_context(tc.psum_pool(name="psum", bufs=1))
         scope.enter_context(tc.manual_schedule())
 
+        w_planes = resident.tile([P, PASSES // PLANES, D], U8, align_bytes=64)
+        for quadrant in (2, 3):
+            first = QUADRANT * quadrant
+            nc.gpsimd.dma_start(
+                out=w_planes[first : first + QUADRANT, 0, :].bitcast(F32),
+                in_=W_b_scales[:, 4 * quadrant : 4 * (quadrant + 1), :].bitcast(F32),
+            )
+        nc.vector.memset(w_planes[P // 2 : P, 1, :].bitcast(I32), 0)
+        nc.vector.memset(w_planes[0 : P // 2].bitcast(I32), 0)
+        for quadrant in (2, 3):
+            first = QUADRANT * quadrant
+            nc.gpsimd.dma_start(
+                out=w_planes[first : first + 4 * PLANES, 1, :].bitcast(F32),
+                in_=W_b_scales[PLANES : 2 * PLANES, 4 * quadrant : 4 * (quadrant + 1), :].bitcast(F32),
+            )
         ident_f32 = resident.tile([P, P], F32)
         make_identity(nc, ident_f32[:])
 
         e_long = resident.tile([P, ROWS_LONG, N], BF16)
         nc.sync.dma_start(out=e_long[:], in_=embedding[0].rearrange("(q r) n -> q r n", q=P))
-
-        w_planes = resident.tile([P, PASSES // PLANES, D], U8, align_bytes=64)
-        nc.vector.memset(w_planes[:].bitcast(I32), 0)
         for four in range(PASSES // PLANES):
             for quadrant in (0, 1):
                 first = QUADRANT * quadrant
@@ -62,15 +74,6 @@ def tile_parallelcoattention_w_kernel(tc, embedding, heatm, W_b_words, W_b_scale
                             PLANES * four : PLANES * (four + 1), 4 * quadrant : 4 * (quadrant + 1), cols
                         ].bitcast(I32),
                     )
-        for four in range(PASSES // PLANES):
-            for quadrant in (2, 3):
-                first = QUADRANT * quadrant
-                nc.gpsimd.dma_start(
-                    out=w_planes[first : first + 4 * PLANES, four, :].bitcast(F32),
-                    in_=W_b_scales[
-                        PLANES * four : PLANES * (four + 1), 4 * quadrant : 4 * (quadrant + 1), :
-                    ].bitcast(F32),
-                )
 
         w_words = {}
         for g in range(EARLY_PASSES):

@@ -66,14 +66,12 @@ def tile_parallelcoattention_w_kernel(tc, embedding, heatm, W_b_words, W_b_scale
         for four in range(PASSES // PLANES):
             for quadrant in (0, 1):
                 first = QUADRANT * quadrant
-                for half in range(2):
-                    cols = slice(half * D // 2, (half + 1) * D // 2)
-                    nc.sync.dma_start(
-                        out=w_planes[first : first + 4 * PLANES, four, cols].bitcast(I32),
-                        in_=W_b_scales[
-                            PLANES * four : PLANES * (four + 1), 4 * quadrant : 4 * (quadrant + 1), cols
-                        ].bitcast(I32),
-                    )
+                nc.sync.dma_start(
+                    out=w_planes[first : first + 4 * PLANES, four, :].bitcast(I32),
+                    in_=W_b_scales[
+                        PLANES * four : PLANES * (four + 1), 4 * quadrant : 4 * (quadrant + 1), :
+                    ].bitcast(I32),
+                )
 
         w_words = {}
         for g in range(EARLY_PASSES):

@@ -58,6 +58,8 @@ def tile_parallelcoattention_w_kernel(tc, embedding, heatm, W_b_words, W_b_scale
                 out=w_planes[first : first + 4 * PLANES, 1, :].bitcast(F32),
                 in_=W_b_scales[PLANES : 2 * PLANES, 4 * quadrant : 4 * (quadrant + 1), :].bitcast(F32),
             )
+        w_first = resident.tile([P, D], U32, name="w_row0", align_bytes=64)
+        nc.gpsimd.memset(w_first[:, 0:16].bitcast(F32), 0.0)
         ident_f32 = resident.tile([P, P], F32)
         make_identity(nc, ident_f32[:])
 
@@ -75,7 +77,7 @@ def tile_parallelcoattention_w_kernel(tc, embedding, heatm, W_b_words, W_b_scale
 
         w_words = {}
         for g in range(EARLY_PASSES):
-            w_row = resident.tile([P, D], U32, name="w_row%d" % g, align_bytes=64)
+            w_row = w_first if g == 0 else resident.tile([P, D], U32, name="w_row%d" % g, align_bytes=64)
             nc.sync.dma_start(
                 out=w_row[:].bitcast(I32),
                 in_=W_b_words[g].rearrange("p n j -> p (n j)").bitcast(I32),

from contextlib import ExitStack

import concourse.mybir as mybir
from concourse.masks import make_identity

F32 = mybir.dt.float32
BF16 = mybir.dt.bfloat16
I32 = mybir.dt.int32
U32 = mybir.dt.uint32
U8 = mybir.dt.uint8
FP8X4 = mybir.dt.float8_e4m3fn_x4
ACT = mybir.ActivationFunctionType
ALU = mybir.AluOpType
AXIS = mybir.AxisListType

P = 128
PACK = 4
HALVES = 2
K_PASS = P * PACK
D = 4096
N = 128
PASSES = D // K_PASS
BLOCK = 512
BLOCKS = D // BLOCK
PAIR = 2
LATE_PASSES = 3
EARLY_PASSES = PASSES - LATE_PASSES
LATE_GROUPS = ((0, 1, 2, 3), (4, 5), (6, 7))
ROWS_LONG = D // P
PAIRS_LONG = ROWS_LONG // 2
PLANES = 4
QUADRANT = 32

FLOPS = 2 * N * D * D + 2 * N * D * N
BYTES = D * N * 2 + D * D + D * D // 32 + N * 4


def tile_parallelcoattention_w_kernel(tc, embedding, heatm, W_b_words, W_b_scales, out):
    nc = tc.nc
    with ExitStack() as scope:
        resident = scope.enter_context(tc.tile_pool(name="resident", bufs=1))
        stage = scope.enter_context(tc.tile_pool(name="stage", bufs=2))
        psum = scope.enter_context(tc.psum_pool(name="psum", bufs=1))
        scope.enter_context(tc.manual_schedule())

        w_planes = resident.tile([P, PASSES // PLANES, D], U8, align_bytes=64)
        for quadrant in (2, 3):
            first = QUADRANT * quadrant
            nc.gpsimd.dma_start(
                out=w_planes[first : first + QUADRANT, 0, :].bitcast(F32),
                in_=W_b_scales[:, 4 * quadrant : 4 * (quadrant + 1), :].bitcast(F32),
            )
        nc.vector.memset(w_planes[P // 2 : P, 1, :].bitcast(I32), 0)
        nc.vector.memset(w_planes[0 : P // 2].bitcast(I32), 0)
        for quadrant in (2, 3):
            first = QUADRANT * quadrant
            nc.gpsimd.dma_start(
                out=w_planes[first : first + 4 * PLANES, 1, :].bitcast(F32),
                in_=W_b_scales[PLANES : 2 * PLANES, 4 * quadrant : 4 * (quadrant + 1), :].bitcast(F32),
            )
        w_first = resident.tile([P, D], U32, name="w_row0", align_bytes=64)
        nc.gpsimd.memset(w_first[:, 0:16].bitcast(F32), 0.0)
        ident_f32 = resident.tile([P, P], F32)
        make_identity(nc, ident_f32[:])

        e_long = resident.tile([P, ROWS_LONG, N], BF16)
        nc.sync.dma_start(out=e_long[:], in_=embedding[0].rearrange("(q r) n -> q r n", q=P))
        for four in range(PASSES // PLANES):
            for quadrant in (0, 1):
                first = QUADRANT * quadrant
                nc.sync.dma_start(
                    out=w_planes[first : first + 4 * PLANES, four, :].bitcast(I32),
                    in_=W_b_scales[
                        PLANES * four : PLANES * (four + 1), 4 * quadrant : 4 * (quadrant + 1), :
                    ].bitcast(I32),
                )

        w_words = {}
        for g in range(EARLY_PASSES):
            w_row = w_first if g == 0 else resident.tile([P, D], U32, name="w_row%d" % g, align_bytes=64)
            nc.sync.dma_start(
                out=w_row[:].bitcast(I32),
                in_=W_b_words[g].rearrange("p n j -> p (n j)").bitcast(I32),
            )
            for c in range(BLOCKS):
                w_words[(g, c)] = w_row[:, BLOCK * c : BLOCK * (c + 1)]
        for group in LATE_GROUPS:
            for g in range(EARLY_PASSES, PASSES):
                very_last = group == LATE_GROUPS[-1] and g == PASSES - 1
                piece_blocks = 1 if very_last else len(group)
                for first in range(group[0], group[-1] + 1, piece_blocks):
                    w_piece = resident.tile(
                        [P, BLOCK * piece_blocks], U32, name="w_piece%d_%d" % (g, first), align_bytes=64
                    )
                    nc.sync.dma_start(
                        out=w_piece[:].bitcast(I32),
                        in_=W_b_words[g]
                        .rearrange("p n j -> p (n j)")[
                            :, PACK * BLOCK * first : PACK * BLOCK * (first + piece_blocks)
                        ]
                        .bitcast(I32),
                    )
                    for b in range(piece_blocks):
                        w_words[(g, first + b)] = w_piece[:, BLOCK * b : BLOCK * (b + 1)]

        warm_in = resident.tile([P, 1], F32)
        nc.vector.memset(warm_in[:], 0.0)
        warm_out = resident.tile([P, 1], F32)
        nc.scalar.activation(out=warm_out[:], in_=warm_in[:], func=ACT.Tanh)

        e_words = e_long[:].rearrange("q r n -> q (r n)").bitcast(F32)
        e_turned = resident.tile([P, P, PAIRS_LONG], F32)
        for b in range(PAIRS_LONG // PACK):
            turned = psum.tile([P, PACK, P], F32, name="turned%d" % b, tag="bank%d" % b)
            for k in range(PACK):
                first_word = P * (PACK * b + k)
                nc.tensor.transpose(turned[:, k, :], e_words[:, first_word : first_word + P], ident_f32[:])
            copy_out = nc.scalar.copy if b % 2 == 0 else nc.vector.tensor_copy
            copy_out(
                out=e_turned[:, :, PACK * b : PACK * (b + 1)], in_=turned[:].rearrange("x k q -> x q k")
            )
        e_flat = e_turned[:].rearrange("x q k -> x (q k)")
        e_grouped = resident.tile([P, PASSES, N, PACK], BF16, align_bytes=64)
        for b in range(PASSES // 2):
            placed = psum.tile([P, 2, HALVES, P], F32, name="placed%d" % b, tag="bank%d" % (4 + b))
            for g in range(2):
                for u in range(HALVES):
                    first_word = 2 * P * (2 * b + g) + u
                    nc.tensor.transpose(
                        placed[:, g, u, :], e_flat[:, first_word : first_word + 2 * P - 1 : 2], ident_f32[:]
                    )
            copy_out = nc.scalar.copy if b % 2 == 0 else nc.vector.tensor_copy
            copy_out(
                out=e_grouped[:, 2 * b : 2 * b + 2],
                in_=placed[:]
                .rearrange("p g u x -> p (g u x)")
                .bitcast(BF16)
                .rearrange("p (g j n) -> p g n j", g=2, j=PACK),
            )

        e_codes = resident.tile([P, PASSES, N], U32, align_bytes=64)
        e_scales = resident.tile([P, PASSES, N], U8, align_bytes=64)
        nc.vector.quantize_mx(
            out=e_codes[:].rearrange("p g n -> p (g n)").bitcast(FP8X4),
            scales=e_scales[:].rearrange("p g n -> p (g n)"),
            in_=e_grouped[:].rearrange("p g n j -> p (g n j)"),
        )

        t_banks = [
            psum.tile([P, BLOCK], F32, name="t_bank%d" % c, tag="bank%d" % c) for c in range(BLOCKS)
        ]
        t_codes = resident.tile([P, PASSES, N], U32, align_bytes=64)
        t_scales = resident.tile([P, PASSES, N], U8, align_bytes=64)
        t_rows = {}

        def t_pass(g, c):
            nc.tensor.matmul_mx(
                out=t_banks[c][:],
                lhsT=e_codes[:, g, :].bitcast(FP8X4),
                lhsT_scale=e_scales[:, g, :],
                rhs=w_words[(g, c)].bitcast(FP8X4),
                rhs_scale=w_planes[
                    4 * (g % PLANES) : P, g // PLANES, BLOCK * c : BLOCK * (c + 1)
                ],
                start=(g == 0),
                stop=(g == PASSES - 1),
            )

        def words_of(pairs):
            return pairs.rearrange("p x i -> p (x i)").bitcast(F32)

        def leave_psum(c, out_tile, in_bank):
            if c % 2 == 0:
                nc.scalar.copy(out=out_tile, in_=in_bank)
            else:
                nc.vector.tensor_copy(out=out_tile, in_=in_bank)

        def round_pair(first):
            for c in range(first, first + PAIR):
                rows = stage.tile([P, HALVES, P, 2], BF16, name="rows%d" % (c % PAIR))
                leave_psum(c, rows[:], t_banks[c][:].rearrange("n (p u i) -> n u p i", u=HALVES, i=2))
                t_rows[c] = rows

        def quantise_pair(first):
            grouped = stage.tile([P, PAIR, N, PACK], BF16, align_bytes=64)
            cols = {}
            for c in range(first, first + PAIR):
                cols[c] = psum.tile([P, HALVES, N], F32, name="cols%d" % c, tag="bank%d" % c)
                for u in range(HALVES):
                    nc.tensor.transpose(cols[c][:, u, :], words_of(t_rows[c][:, u]), ident_f32[:])
            for c in range(first, first + PAIR):
                leave_psum(
                    c,
                    words_of(grouped[:, c - first]).rearrange("p (n u) -> p n u", u=HALVES),
                    cols[c][:].rearrange("p u n -> p n u"),
                )
            nc.vector.quantize_mx(
                out=t_codes[:, first : first + PAIR, :]
                .rearrange("p c n -> p (c n)")
                .bitcast(FP8X4),
                scales=t_scales[:, first : first + PAIR, :].rearrange("p c n -> p (c n)"),
                in_=grouped[:].rearrange("p c n j -> p (c n j)"),
            )

        def scores_pass(scores, c):
            nc.tensor.matmul_mx(
                out=scores[:],
                lhsT=t_codes[:, c, :].bitcast(FP8X4),
                lhsT_scale=t_scales[:, c, :],
                rhs=e_codes[:, c, :].bitcast(FP8X4),
                rhs_scale=e_scales[:, c, :],
                start=(c == 0),
                stop=(c == BLOCKS - 1),
            )

        for g in range(EARLY_PASSES):
            for c in range(BLOCKS):
                t_pass(g, c)

        score_tiles = []

        def scores_pair(first):
            if not score_tiles:
                score_tiles.append(psum.tile([P, N], F32, name="scores", tag="bank0"))
            for c in range(first, first + PAIR):
                scores_pass(score_tiles[0], c)

        owed = []
        for group in LATE_GROUPS:
            for late in range(LATE_PASSES):
                for c in group:
                    t_pass(EARLY_PASSES + late, c)
                very_last = group == LATE_GROUPS[-1] and late == LATE_PASSES - 1
                for step, first in owed[: len(owed) if very_last else 1]:
                    step(first)
                owed = [] if very_last else owed[1:]
            if group != LATE_GROUPS[-1]:
                for first in group[::PAIR]:
                    round_pair(first)
                owed = (
                    [item for item in owed if item[0] == quantise_pair]
                    + [(quantise_pair, first) for first in group[::PAIR]]
                    + [item for item in owed if item[0] == scores_pair]
                    + [(scores_pair, first) for first in group[::PAIR]]
                )
        scores = score_tiles[0]

        c_a, c_b = BLOCKS - 2, BLOCKS - 1
        rows_a = stage.tile([P, HALVES, P, 2], BF16, name="rows0")
        rows_b = stage.tile([P, HALVES, P, 2], BF16, name="rows1")
        sums_a = t_banks[c_a][:].rearrange("n (p u i) -> n u p i", u=HALVES, i=2)
        sums_b = t_banks[c_b][:].rearrange("n (p u i) -> n u p i", u=HALVES, i=2)
        nc.scalar.copy(out=rows_a[:], in_=sums_a)
        for u in range(HALVES):
            nc.vector.tensor_copy(out=rows_b[:, u], in_=sums_b[:, u])
        cols_a = psum.tile([P, HALVES, N], F32, name="cols_a", tag="bank%d" % c_a)
        cols_b = psum.tile([P, HALVES, N], F32, name="cols_b", tag="bank%d" % (c_b - 3))
        for u in range(HALVES):
            nc.tensor.transpose(cols_a[:, u, :], words_of(rows_a[:, u]), ident_f32[:])
        for u in range(HALVES):
            nc.tensor.transpose(cols_b[:, u, :], words_of(rows_b[:, u]), ident_f32[:])
        grouped_a = resident.tile([P, N, PACK], BF16, align_bytes=64)
        grouped_b = resident.tile([P, N, PACK], BF16, align_bytes=64)
        nc.scalar.copy(
            out=words_of(grouped_a[:]).rearrange("p (n u) -> p n u", u=HALVES),
            in_=cols_a[:].rearrange("p u n -> p n u"),
        )
        nc.vector.tensor_copy(
            out=words_of(grouped_b[:]).rearrange("p (n u) -> p n u", u=HALVES),
            in_=cols_b[:].rearrange("p u n -> p n u"),
        )
        for c, grouped in ((c_a, grouped_a), (c_b, grouped_b)):
            nc.vector.quantize_mx(
                out=t_codes[:, c, :].bitcast(FP8X4),
                scales=t_scales[:, c, :],
                in_=grouped[:].rearrange("p n j -> p (n j)"),
            )
        scores_pass(scores, c_a)
        scores_pass(scores, c_b)

        row_max = resident.tile([P, 1], F32)
        nc.vector.reduce_max(out=row_max[:], in_=scores[:], axis=AXIS.X)
        spread_v = psum.tile([P, N], F32, tag="bank1")
        spread_s = psum.tile([P, N], F32, tag="bank2")
        nc.tensor.transpose(spread_v[:], row_max[:, 0:1].to_broadcast([P, P]), ident_f32[:])
        nc.tensor.transpose(spread_s[:], row_max[:, 0:1].to_broadcast([P, P]), ident_f32[:])
        neg_raw_top = resident.tile([P, 1], F32)
        nc.vector.tensor_reduce(
            out=neg_raw_top[:], in_=spread_v[:], axis=AXIS.X, op=ALU.max, negate=True
        )
        c_max = resident.tile([P, N], F32)
        nc.scalar.activation(out=c_max[:], in_=spread_s[:], func=ACT.Tanh)
        neg_top = resident.tile([P, 1], F32)
        nc.scalar.activation(out=neg_top[:], in_=neg_raw_top[:], func=ACT.Tanh)
        powers = resident.tile([P, N], F32)
        total = resident.tile([P, 1], F32)
        nc.scalar.activation(
            out=powers[:], in_=c_max[:], func=ACT.Exp, bias=neg_top[:, 0:1], accum_out=total[:]
        )
        inverse = resident.tile([P, 1], F32)
        nc.vector.reciprocal(out=inverse[:], in_=total[:])
        weights = resident.tile([P, N], F32)
        nc.vector.tensor_scalar_mul(out=weights[:], in0=powers[:], scalar1=inverse[:, 0:1])
        nc.sync.dma_start(out=out.rearrange("b n o -> (b o) n"), in_=weights[0:1, :])
